import numpy as np
import ml_dtypes


def mxq(x, axis, fmt="e4m3"):
    dtype, down = {"e4m3": (ml_dtypes.float8_e4m3fn, 7), "e5m2": (ml_dtypes.float8_e5m2, 14)}[fmt]
    v = np.moveaxis(np.asarray(x, np.float32).astype(ml_dtypes.bfloat16).astype(np.float64), axis, -1)
    blocks = v.reshape(v.shape[:-1] + (-1, 32))
    amax = np.abs(blocks).max(-1, keepdims=True)
    byte = np.maximum(np.where(amax > 0, np.frexp(amax)[1] - 1 + 127, 0) - down, 1)
    scale = np.exp2(byte - 127.0)
    codes = (blocks / scale).astype(np.float32).astype(dtype).astype(np.float64)
    return np.moveaxis((codes * scale).reshape(v.shape), -1, axis)


WIDE = False


def mx_kscale(k):
    if not WIDE:
        return np.ones(k)
    levels = np.array([10, -10, 5, -5, 0])
    a = np.random.permutation(np.resize(levels, k // 512 * 4)).reshape(k // 512, 4)
    idx = np.arange(k)
    return np.exp2(a[idx // 512, idx % 128 // 32])


BF16 = ml_dtypes.bfloat16


def bf(x):
    return np.asarray(x, np.float32).astype(BF16)


def f64(x):
    return np.asarray(x).astype(np.float64)


B, N, D = 4, 512, 512
C = 2 * D
EPS_BN = 1e-5
NEG_SLOPE = 0.01


def bn_lrelu(x, g, b):
    mean = np.mean(x, axis=(0, 2), keepdims=True)
    var = np.var(x, axis=(0, 2), keepdims=True)
    y = (x - mean) / np.sqrt(var + EPS_BN) * g[None, :, None] + b[None, :, None]
    return np.where(y >= 0, y, NEG_SLOPE * y)


def setup_inputs():
    s = mx_kscale(C)
    v = np.random.standard_normal((B, C, N))
    return {"h1": bf(np.where(v >= 0, v, NEG_SLOPE * v) * s[None, :, None]),
            "W2": bf(np.random.standard_normal((D, C)) / np.sqrt(C) / s[None, :]),
            "g2": bf(1.0 + 0.2 * np.random.standard_normal(D)),
            "b2": bf(0.3 * np.random.standard_normal(D))}


def reference(h1, W2, g2, b2):
    z = mxq(f64(W2), 1, "e4m3") @ mxq(f64(h1), 1, "e4m3")
    return np.swapaxes(bn_lrelu(z, f64(g2), f64(b2)), 1, 2)

@@ -1,0 +1,220 @@
+from contextlib import ExitStack
+
+import concourse.masks as masks
+import concourse.mybir as mybir
+
+F32 = mybir.dt.float32
+BF16 = mybir.dt.bfloat16
+U32 = mybir.dt.uint32
+U8 = mybir.dt.uint8
+FP8X4 = mybir.dt.float8_e4m3fn_x4
+ACT = mybir.ActivationFunctionType
+ALU = mybir.AluOpType
+
+P = 128
+B, C, N, D = 4, 1024, 512, 512
+G = C // 512
+OT = D // P
+NJ = N // P
+EPS_BN = 1e-5
+NEG_SLOPE = 0.01
+FLOPS = 2 * B * D * N * C
+
+VCOLS = [512, 512, 256, 0, 0, 0, 0, 0]
+STATS_LAG = 1
+STATS_PER_STEP = 3
+PIN = True
+
+
+def tile_yuyipointupdate_pb_kernel(tc, h1, W2, g2, b2, out):
+    nc = tc.nc
+    with ExitStack() as ctx:
+        keep = ctx.enter_context(tc.tile_pool(name="keep", bufs=1))
+        apool = ctx.enter_context(tc.tile_pool(name="apool", bufs=4))
+        psum = ctx.enter_context(tc.psum_pool(name="psum", bufs=1))
+        if PIN:
+            ctx.enter_context(tc.manual_schedule())
+
+        def bank(i, shape, name):
+            return psum.tile(shape, F32, tag="bank%d" % i, name=name)
+
+        gbraw = keep.tile([P, P], BF16, name="gbraw")
+        nc.vector.memset(gbraw[:], 0.0)
+        nc.scalar.dma_start(out=gbraw[0:OT, :], in_=g2.rearrange("(t p) -> t p", p=P))
+        nc.scalar.dma_start(out=gbraw[OT : 2 * OT, :], in_=b2.rearrange("(t p) -> t p", p=P))
+        one = keep.tile([P, 1], F32, name="one")
+        nc.vector.memset(one[:], 1.0)
+        warm = keep.tile([P, 1], F32, name="warm")
+        nc.scalar.activation(out=warm[:], in_=one[:], func=ACT.Sqrt)
+        ident = keep.tile([P, P], F32, name="ident")
+        masks.make_identity(nc, ident[:])
+
+        w2raw = keep.tile([P, OT, C], BF16, name="w2raw")
+        w2view = W2.rearrange("(t p) c -> p t c", p=P)
+        h1view = h1.rearrange("b (g p j) n -> b g p j n", g=G, p=P, j=4)
+        h1raw = [keep.tile([P, 4, N], BF16, name="h1raw%d" % k) for k in range(B * G)]
+        nc.sync.dma_start(out=h1raw[0][:], in_=h1view[0, 0])
+        nc.sync.dma_start(out=w2raw[:, 0:2, :], in_=w2view[:, 0:2, :])
+        nc.sync.dma_start(out=w2raw[:, 2:4, :], in_=w2view[:, 2:4, :])
+        for k in range(1, B * G):
+            nc.sync.dma_start(out=h1raw[k][:], in_=h1view[k // G, k % G])
+
+        gbf = keep.tile([P, P], F32, name="gbf")
+        gb = keep.tile([P, 2 * OT], F32, name="gb")
+
+        w2grp = keep.tile([P, OT, G, P, 4], BF16, name="w2grp", align_bytes=64)
+        w2codes = keep.tile([P, OT, G, P], U32, name="w2codes", align_bytes=64)
+        w2scales = keep.tile([P, OT, G, P], U8, name="w2scales", align_bytes=64)
+        w2words = w2raw[:].bitcast(F32).rearrange("p t (g q u) -> p t g u q", g=G, u=2)
+        w2grpw = w2grp[:].bitcast(F32)
+
+        def w2_stage():
+            nc.vector.tensor_copy(out=gbf[:], in_=gbraw[:])
+            for ot in range(OT):
+                wt = bank(ot, [P, G, 2, P], "wt%d" % ot)
+                for g in range(G):
+                    for u in range(2):
+                        nc.tensor.transpose(wt[:, g, u, :], w2words[:, ot, g, u, :], ident[:])
+                nc.scalar.copy(out=w2grpw[:, ot], in_=wt[:].rearrange("p g u o -> p g o u"))
+            gbps = bank(4, [P, P], "gbps")
+            nc.tensor.transpose(gbps[:], gbf[:], ident[:])
+            for ot in range(OT):
+                nc.vector.quantize_mx(
+                    out=w2codes[:, ot].rearrange("p g o -> p (g o)").bitcast(FP8X4),
+                    scales=w2scales[:, ot].rearrange("p g o -> p (g o)"),
+                    in_=w2grp[:, ot].rearrange("p g o t -> p (g o t)"),
+                )
+            nc.vector.tensor_copy(out=gb[:], in_=gbps[:, 0 : 2 * OT])
+
+        h1codes = keep.tile([P, B * G, N], U32, name="h1codes", align_bytes=64)
+        h1scales = keep.tile([P, B * G, N], U8, name="h1scales", align_bytes=64)
+        grps = [keep.tile([P, N, 4], BF16, name="h1grp%d" % k, align_bytes=64) for k in range(B * G)]
+
+        def regroup(k):
+            dst = grps[k][:].rearrange("p (c i) t -> p c t i", i=4)
+            src = h1raw[k][:].rearrange("p t (c i) -> p c t i", i=4)
+            cv = VCOLS[k] // 4
+            if cv > 0:
+                nc.vector.tensor_copy(out=dst[:, 0:cv], in_=src[:, 0:cv])
+            if cv < N // 4:
+                nc.scalar.copy(out=dst[:, cv:], in_=src[:, cv:])
+
+        def quantise(k):
+            nc.vector.quantize_mx(
+                out=h1codes[:, k, :].bitcast(FP8X4),
+                scales=h1scales[:, k, :],
+                in_=grps[k][:].rearrange("p n t -> p (n t)"),
+            )
+
+        def mx_pass(z, b, ot, g):
+            nc.tensor.matmul_mx(
+                out=z[:],
+                lhsT=w2codes[:, ot, g, :].bitcast(FP8X4),
+                lhsT_scale=w2scales[:, ot, g, :],
+                rhs=h1codes[:, b * G + g, :].bitcast(FP8X4),
+                rhs_scale=h1scales[:, b * G + g, :],
+                start=(g == 0),
+                stop=(g == G - 1),
+            )
+
+        stats = keep.tile([P, OT, B, 6], F32, name="stats")
+        held = {}
+        units = []
+        taken = 0
+        for k in range(B * G + 1):
+            if k < B * G:
+                regroup(k)
+            if k == 1:
+                w2_stage()
+            if k >= 1:
+                c = k - 1
+                b, g = c // G, c % G
+                quantise(c)
+                if g == 0:
+                    base = 4 if b % 2 == 0 else 0
+                    held[b] = [bank(base + ot, [P, N], "z%d_%d" % (b, ot)) for ot in range(OT)]
+                for ot in range(OT):
+                    mx_pass(held[b][ot], b, ot, g)
+                if g == G - 1:
+                    units.extend([(c, b, ot) for ot in range(OT)])
+            last = k == B * G
+            for w in units[taken : (len(units) if last else taken + STATS_PER_STEP)]:
+                if last or w[0] <= k - 1 - STATS_LAG:
+                    nc.vector.bn_stats(out=stats[:, w[2], w[1], :], in_=held[w[1]][w[2]][:])
+                    taken += 1
+
+        mv = keep.tile([P, OT, 2], F32, name="mv")
+        for ot in range(OT):
+            nc.vector.bn_aggr(out=mv[:, ot, :], in_=stats[:, ot].rearrange("p b s -> p (b s)"))
+        sd = keep.tile([P, OT], F32, name="sd")
+        nc.scalar.activation(out=sd[:], in_=mv[:, :, 1], func=ACT.Sqrt, bias=EPS_BN, scale=1.0)
+        rstd = keep.tile([P, OT], F32, name="rstd")
+        nc.vector.reciprocal(out=rstd[:], in_=sd[:])
+        sc = keep.tile([P, OT], F32, name="sc")
+        nc.vector.tensor_tensor(out=sc[:], in0=gb[:, 0:OT], in1=rstd[:], op=ALU.mult)
+        ms = keep.tile([P, OT], F32, name="ms")
+        nc.vector.tensor_tensor(out=ms[:], in0=mv[:, :, 0], in1=sc[:], op=ALU.mult)
+        sh = keep.tile([P, OT], F32, name="sh")
+        nc.vector.tensor_tensor(out=sh[:], in0=gb[:, OT : 2 * OT], in1=ms[:], op=ALU.subtract)
+
+        ys = {}
+
+        def normalise(b, zs):
+            for ot in range(OT):
+                y = keep.tile([P, N], F32, name="y%d_%d" % (b, ot))
+                if ot < 2:
+                    nc.scalar.activation(
+                        out=y[:], in_=zs[ot][:], func=ACT.Identity,
+                        bias=sh[:, ot : ot + 1], scale=sc[:, ot : ot + 1],
+                    )
+                else:
+                    nc.vector.tensor_scalar(
+                        out=y[:], in0=zs[ot][:], scalar1=sc[:, ot : ot + 1],
+                        scalar2=sh[:, ot : ot + 1], op0=ALU.mult, op1=ALU.add,
+                    )
+                ys[(b, ot)] = y
+
+        def recompute(b):
+            zs = [bank(ot, [P, N], "zr%d_%d" % (b, ot)) for ot in range(OT)]
+            for ot in range(OT):
+                for g in range(G):
+                    mx_pass(zs[ot], b, ot, g)
+            return zs
+
+        def transposes(b):
+            ts = []
+            for j in range(NJ):
+                t = bank(4 + j, [P, D], "t%d_%d" % (b, j))
+                for ot in range(OT):
+                    nc.tensor.transpose(
+                        t[:, ot * P : (ot + 1) * P], ys[(b, ot)][:, j * P : (j + 1) * P], ident[:]
+                    )
+                ts.append(t)
+            return ts
+
+        outview = out.rearrange("b (j p) o -> b j p o", p=P)
+
+        def finish(b, ts):
+            for j in range(NJ):
+                a = apool.tile([P, D], F32, name="a")
+                nc.scalar.copy(out=a[:], in_=ts[j][:])
+                r = keep.tile([P, D], F32, name="r%d_%d" % (b, j))
+                nc.vector.scalar_tensor_tensor(
+                    out=r[:], in0=ts[j][:], scalar=NEG_SLOPE, in1=a[:], op0=ALU.mult, op1=ALU.max
+                )
+                nc.sync.dma_start(out=outview[b, j], in_=r[:])
+
+        normalise(2, held[2])
+        normalise(3, held[3])
+        t2 = transposes(2)
+        z0 = recompute(0)
+        finish(2, t2)
+        normalise(0, z0)
+        t3 = transposes(3)
+        z1 = recompute(1)
+        finish(3, t3)
+        normalise(1, z1)
+        t0 = transposes(0)
+        finish(0, t0)
+        t1 = transposes(1)
+        finish(1, t1)

@@ -24,6 +24,9 @@ VCOLS = [512, 512, 256, 0, 0, 0, 0, 0]
 STATS_LAG = 1
 STATS_PER_STEP = 3
 PIN = True
+ORDER = [2, 3, 0, 1]
+P2_ON_VECTOR = [2, 3, 2, 2]
+G_BANK = 3
 
 
 def tile_yuyipointupdate_pb_kernel(tc, h1, W2, g2, b2, out):
@@ -31,6 +34,7 @@ def tile_yuyipointupdate_pb_kernel(tc, h1, W2, g2, b2, out):
     with ExitStack() as ctx:
         keep = ctx.enter_context(tc.tile_pool(name="keep", bufs=1))
         apool = ctx.enter_context(tc.tile_pool(name="apool", bufs=4))
+        gpool = ctx.enter_context(tc.tile_pool(name="gpool", bufs=2))
         psum = ctx.enter_context(tc.psum_pool(name="psum", bufs=1))
         if PIN:
             ctx.enter_context(tc.manual_schedule())
@@ -162,7 +166,7 @@ def tile_yuyipointupdate_pb_kernel(tc, h1, W2, g2, b2, out):
         def normalise(b, zs):
             for ot in range(OT):
                 y = keep.tile([P, N], F32, name="y%d_%d" % (b, ot))
-                if ot < 2:
+                if ot < OT - P2_ON_VECTOR[ORDER.index(b)]:
                     nc.scalar.activation(
                         out=y[:], in_=zs[ot][:], func=ACT.Identity,
                         bias=sh[:, ot : ot + 1], scale=sc[:, ot : ot + 1],
@@ -194,15 +198,34 @@ def tile_yuyipointupdate_pb_kernel(tc, h1, W2, g2, b2, out):
 
         outview = out.rearrange("b (j p) o -> b j p o", p=P)
 
+        gres = {}
+
         def finish(b, ts):
             for j in range(NJ):
-                a = apool.tile([P, D], F32, name="a")
-                nc.scalar.copy(out=a[:], in_=ts[j][:])
                 r = keep.tile([P, D], F32, name="r%d_%d" % (b, j))
-                nc.vector.scalar_tensor_tensor(
-                    out=r[:], in0=ts[j][:], scalar=NEG_SLOPE, in1=a[:], op0=ALU.mult, op1=ALU.max
-                )
-                nc.sync.dma_start(out=outview[b, j], in_=r[:])
+                if j == G_BANK and b != ORDER[-1]:
+                    ag = gpool.tile([P, D], F32, name="ag")
+                    nc.scalar.copy(out=ag[:], in_=ts[j][:])
+                    neg = gpool.tile([P, D], F32, name="neg")
+                    nc.gpsimd.tensor_scalar(
+                        out=neg[:], in0=ag[:], scalar1=0.0, scalar2=-3.0e38, op0=ALU.min, op1=ALU.max
+                    )
+                    nc.gpsimd.tensor_scalar(
+                        out=neg[:], in0=neg[:], scalar1=NEG_SLOPE - 1.0, scalar2=0.0,
+                        op0=ALU.mult, op1=ALU.add,
+                    )
+                    nc.gpsimd.tensor_tensor(out=r[:], in0=ag[:], in1=neg[:], op=ALU.add)
+                    gres[b] = r
+                else:
+                    a = apool.tile([P, D], F32, name="a")
+                    nc.scalar.copy(out=a[:], in_=ts[j][:])
+                    nc.vector.scalar_tensor_tensor(
+                        out=r[:], in0=ts[j][:], scalar=NEG_SLOPE, in1=a[:], op0=ALU.mult, op1=ALU.max
+                    )
+                    nc.sync.dma_start(out=outview[b, j], in_=r[:])
+                if j == 1 and b != ORDER[0]:
+                    before = ORDER[ORDER.index(b) - 1]
+                    nc.sync.dma_start(out=outview[before, G_BANK], in_=gres[before][:])
 
         normalise(2, held[2])
         normalise(3, held[3])

@@ -24,9 +24,6 @@ VCOLS = [512, 512, 256, 0, 0, 0, 0, 0]
 STATS_LAG = 1
 STATS_PER_STEP = 3
 PIN = True
-ORDER = [2, 3, 0, 1]
-P2_ON_VECTOR = [2, 3, 2, 2]
-G_BANK = 3
 
 
 def tile_yuyipointupdate_pb_kernel(tc, h1, W2, g2, b2, out):
@@ -34,7 +31,6 @@ def tile_yuyipointupdate_pb_kernel(tc, h1, W2, g2, b2, out):
     with ExitStack() as ctx:
         keep = ctx.enter_context(tc.tile_pool(name="keep", bufs=1))
         apool = ctx.enter_context(tc.tile_pool(name="apool", bufs=4))
-        gpool = ctx.enter_context(tc.tile_pool(name="gpool", bufs=2))
         psum = ctx.enter_context(tc.psum_pool(name="psum", bufs=1))
         if PIN:
             ctx.enter_context(tc.manual_schedule())
@@ -122,6 +118,11 @@ def tile_yuyipointupdate_pb_kernel(tc, h1, W2, g2, b2, out):
             )
 
         stats = keep.tile([P, OT, B, 6], F32, name="stats")
+        mv = keep.tile([P, OT, 2], F32, name="mv")
+
+        def aggregate(ot):
+            nc.vector.bn_aggr(out=mv[:, ot, :], in_=stats[:, ot].rearrange("p b s -> p (b s)"))
+
         held = {}
         units = []
         taken = 0
@@ -146,27 +147,31 @@ def tile_yuyipointupdate_pb_kernel(tc, h1, W2, g2, b2, out):
                 if last or w[0] <= k - 1 - STATS_LAG:
                     nc.vector.bn_stats(out=stats[:, w[2], w[1], :], in_=held[w[1]][w[2]][:])
                     taken += 1
+                    if w[1] == B - 1 and w[2] > 0:
+                        aggregate(w[2] - 1)
+        aggregate(OT - 1)
 
-        mv = keep.tile([P, OT, 2], F32, name="mv")
-        for ot in range(OT):
-            nc.vector.bn_aggr(out=mv[:, ot, :], in_=stats[:, ot].rearrange("p b s -> p (b s)"))
         sd = keep.tile([P, OT], F32, name="sd")
         nc.scalar.activation(out=sd[:], in_=mv[:, :, 1], func=ACT.Sqrt, bias=EPS_BN, scale=1.0)
+        mg = keep.tile([P, OT], F32, name="mg")
+        nc.vector.scalar_tensor_tensor(
+            out=mg[:], in0=mv[:, :, 0], scalar=-1.0, in1=gb[:, 0:OT], op0=ALU.mult, op1=ALU.mult
+        )
         rstd = keep.tile([P, OT], F32, name="rstd")
         nc.vector.reciprocal(out=rstd[:], in_=sd[:])
+        ms = keep.tile([P, OT], F32, name="ms")
+        nc.vector.tensor_tensor(out=ms[:], in0=mg[:], in1=rstd[:], op=ALU.mult)
         sc = keep.tile([P, OT], F32, name="sc")
         nc.vector.tensor_tensor(out=sc[:], in0=gb[:, 0:OT], in1=rstd[:], op=ALU.mult)
-        ms = keep.tile([P, OT], F32, name="ms")
-        nc.vector.tensor_tensor(out=ms[:], in0=mv[:, :, 0], in1=sc[:], op=ALU.mult)
         sh = keep.tile([P, OT], F32, name="sh")
-        nc.vector.tensor_tensor(out=sh[:], in0=gb[:, OT : 2 * OT], in1=ms[:], op=ALU.subtract)
+        nc.vector.tensor_tensor(out=sh[:], in0=ms[:], in1=gb[:, OT : 2 * OT], op=ALU.add)
 
         ys = {}
 
         def normalise(b, zs):
             for ot in range(OT):
                 y = keep.tile([P, N], F32, name="y%d_%d" % (b, ot))
-                if ot < OT - P2_ON_VECTOR[ORDER.index(b)]:
+                if ot < 2:
                     nc.scalar.activation(
                         out=y[:], in_=zs[ot][:], func=ACT.Identity,
                         bias=sh[:, ot : ot + 1], scale=sc[:, ot : ot + 1],
@@ -185,47 +190,36 @@ def tile_yuyipointupdate_pb_kernel(tc, h1, W2, g2, b2, out):
                     mx_pass(zs[ot], b, ot, g)
             return zs
 
-        def transposes(b):
+        def transposes(b, last=False):
             ts = []
             for j in range(NJ):
-                t = bank(4 + j, [P, D], "t%d_%d" % (b, j))
-                for ot in range(OT):
-                    nc.tensor.transpose(
-                        t[:, ot * P : (ot + 1) * P], ys[(b, ot)][:, j * P : (j + 1) * P], ident[:]
-                    )
-                ts.append(t)
+                halves = 2 if (last and j == NJ - 1) else 1
+                pieces = []
+                for h in range(halves):
+                    width = D // halves
+                    t = bank(4 + j if h == 0 else 0, [P, width], "t%d_%d_%d" % (b, j, h))
+                    for q in range(width // P):
+                        ot = h * (width // P) + q
+                        nc.tensor.transpose(
+                            t[:, q * P : (q + 1) * P], ys[(b, ot)][:, j * P : (j + 1) * P], ident[:]
+                        )
+                    pieces.append((t, h * width, (h + 1) * width))
+                ts.append(pieces)
             return ts
 
         outview = out.rearrange("b (j p) o -> b j p o", p=P)
 
-        gres = {}
-
         def finish(b, ts):
             for j in range(NJ):
+                a = apool.tile([P, D], F32, name="a")
                 r = keep.tile([P, D], F32, name="r%d_%d" % (b, j))
-                if j == G_BANK and b != ORDER[-1]:
-                    ag = gpool.tile([P, D], F32, name="ag")
-                    nc.scalar.copy(out=ag[:], in_=ts[j][:])
-                    neg = gpool.tile([P, D], F32, name="neg")
-                    nc.gpsimd.tensor_scalar(
-                        out=neg[:], in0=ag[:], scalar1=0.0, scalar2=-3.0e38, op0=ALU.min, op1=ALU.max
-                    )
-                    nc.gpsimd.tensor_scalar(
-                        out=neg[:], in0=neg[:], scalar1=NEG_SLOPE - 1.0, scalar2=0.0,
-                        op0=ALU.mult, op1=ALU.add,
-                    )
-                    nc.gpsimd.tensor_tensor(out=r[:], in0=ag[:], in1=neg[:], op=ALU.add)
-                    gres[b] = r
-                else:
-                    a = apool.tile([P, D], F32, name="a")
-                    nc.scalar.copy(out=a[:], in_=ts[j][:])
+                for t, lo, hi in ts[j]:
+                    nc.scalar.copy(out=a[:, lo:hi], in_=t[:])
                     nc.vector.scalar_tensor_tensor(
-                        out=r[:], in0=ts[j][:], scalar=NEG_SLOPE, in1=a[:], op0=ALU.mult, op1=ALU.max
+                        out=r[:, lo:hi], in0=t[:], scalar=NEG_SLOPE, in1=a[:, lo:hi],
+                        op0=ALU.mult, op1=ALU.max,
                     )
-                    nc.sync.dma_start(out=outview[b, j], in_=r[:])
-                if j == 1 and b != ORDER[0]:
-                    before = ORDER[ORDER.index(b) - 1]
-                    nc.sync.dma_start(out=outview[before, G_BANK], in_=gres[before][:])
+                    nc.sync.dma_start(out=outview[b, j][:, lo:hi], in_=r[:, lo:hi])
 
         normalise(2, held[2])
         normalise(3, held[3])
@@ -239,5 +233,5 @@ def tile_yuyipointupdate_pb_kernel(tc, h1, W2, g2, b2, out):
         normalise(1, z1)
         t0 = transposes(0)
         finish(0, t0)
-        t1 = transposes(1)
+        t1 = transposes(1, last=True)
         finish(1, t1)

@@ -20,9 +20,10 @@ EPS_BN = 1e-5
 NEG_SLOPE = 0.01
 FLOPS = 2 * B * D * N * C
 
-VCOLS = [512, 512, 256, 0, 0, 0, 0, 0]
+VCOLS = [512, 512, 384, 256, 0, 0, 0, 0]
 STATS_LAG = 1
-STATS_PER_STEP = 3
+STATS_PER_STEP = 2
+SAVED = [2, 3]
 PIN = True
 
 
@@ -124,6 +125,14 @@ def tile_yuyipointupdate_pb_kernel(tc, h1, W2, g2, b2, out):
             nc.vector.bn_aggr(out=mv[:, ot, :], in_=stats[:, ot].rearrange("p b s -> p (b s)"))
 
         held = {}
+        saved = {}
+
+        def save(b):
+            for ot in range(OT):
+                zs = keep.tile([P, N], F32, name="zs%d_%d" % (b, ot))
+                nc.scalar.copy(out=zs[:], in_=held[b][ot][:])
+                saved[(b, ot)] = zs
+
         units = []
         taken = 0
         for k in range(B * G + 1):
@@ -143,13 +152,28 @@ def tile_yuyipointupdate_pb_kernel(tc, h1, W2, g2, b2, out):
                 if g == G - 1:
                     units.extend([(c, b, ot) for ot in range(OT)])
             last = k == B * G
+            if k == B * G - 1:
+                save(2)
+            if last:
+                save(3)
             for w in units[taken : (len(units) if last else taken + STATS_PER_STEP)]:
                 if last or w[0] <= k - 1 - STATS_LAG:
-                    nc.vector.bn_stats(out=stats[:, w[2], w[1], :], in_=held[w[1]][w[2]][:])
+                    src = saved[(w[1], w[2])] if w[1] in SAVED else held[w[1]][w[2]]
+                    nc.vector.bn_stats(out=stats[:, w[2], w[1], :], in_=src[:])
                     taken += 1
                     if w[1] == B - 1 and w[2] > 0:
                         aggregate(w[2] - 1)
         aggregate(OT - 1)
+
+        def recompute(b, base):
+            zs = [bank(base + ot, [P, N], "zr%d_%d" % (b, ot)) for ot in range(OT)]
+            for ot in range(OT):
+                for g in range(G):
+                    mx_pass(zs[ot], b, ot, g)
+            return zs
+
+        z1 = recompute(1, 4)
+        z0 = recompute(0, 0)
 
         sd = keep.tile([P, OT], F32, name="sd")
         nc.scalar.activation(out=sd[:], in_=mv[:, :, 1], func=ACT.Sqrt, bias=EPS_BN, scale=1.0)
@@ -171,7 +195,7 @@ def tile_yuyipointupdate_pb_kernel(tc, h1, W2, g2, b2, out):
         def normalise(b, zs):
             for ot in range(OT):
                 y = keep.tile([P, N], F32, name="y%d_%d" % (b, ot))
-                if ot < 2:
+                if ot < OT - 1:
                     nc.scalar.activation(
                         out=y[:], in_=zs[ot][:], func=ACT.Identity,
                         bias=sh[:, ot : ot + 1], scale=sc[:, ot : ot + 1],
@@ -183,28 +207,24 @@ def tile_yuyipointupdate_pb_kernel(tc, h1, W2, g2, b2, out):
                     )
                 ys[(b, ot)] = y
 
-        def recompute(b):
-            zs = [bank(ot, [P, N], "zr%d_%d" % (b, ot)) for ot in range(OT)]
+        def normalise_saved(b):
             for ot in range(OT):
-                for g in range(G):
-                    mx_pass(zs[ot], b, ot, g)
-            return zs
+                y = keep.tile([P, N], F32, name="y%d_%d" % (b, ot))
+                nc.vector.tensor_scalar(
+                    out=y[:], in0=saved[(b, ot)][:], scalar1=sc[:, ot : ot + 1],
+                    scalar2=sh[:, ot : ot + 1], op0=ALU.mult, op1=ALU.add,
+                )
+                ys[(b, ot)] = y
 
-        def transposes(b, last=False):
+        def transposes(b, base):
             ts = []
             for j in range(NJ):
-                halves = 2 if (last and j == NJ - 1) else 1
-                pieces = []
-                for h in range(halves):
-                    width = D // halves
-                    t = bank(4 + j if h == 0 else 0, [P, width], "t%d_%d_%d" % (b, j, h))
-                    for q in range(width // P):
-                        ot = h * (width // P) + q
-                        nc.tensor.transpose(
-                            t[:, q * P : (q + 1) * P], ys[(b, ot)][:, j * P : (j + 1) * P], ident[:]
-                        )
-                    pieces.append((t, h * width, (h + 1) * width))
-                ts.append(pieces)
+                t = bank(base + j, [P, D], "t%d_%d" % (b, j))
+                for ot in range(OT):
+                    nc.tensor.transpose(
+                        t[:, ot * P : (ot + 1) * P], ys[(b, ot)][:, j * P : (j + 1) * P], ident[:]
+                    )
+                ts.append(t)
             return ts
 
         outview = out.rearrange("b (j p) o -> b j p o", p=P)
@@ -212,26 +232,22 @@ def tile_yuyipointupdate_pb_kernel(tc, h1, W2, g2, b2, out):
         def finish(b, ts):
             for j in range(NJ):
                 a = apool.tile([P, D], F32, name="a")
+                nc.scalar.copy(out=a[:], in_=ts[j][:])
                 r = keep.tile([P, D], F32, name="r%d_%d" % (b, j))
-                for t, lo, hi in ts[j]:
-                    nc.scalar.copy(out=a[:, lo:hi], in_=t[:])
-                    nc.vector.scalar_tensor_tensor(
-                        out=r[:, lo:hi], in0=t[:], scalar=NEG_SLOPE, in1=a[:, lo:hi],
-                        op0=ALU.mult, op1=ALU.max,
-                    )
-                    nc.sync.dma_start(out=outview[b, j][:, lo:hi], in_=r[:, lo:hi])
+                nc.vector.scalar_tensor_tensor(
+                    out=r[:], in0=ts[j][:], scalar=NEG_SLOPE, in1=a[:], op0=ALU.mult, op1=ALU.max
+                )
+                nc.sync.dma_start(out=outview[b, j], in_=r[:])
 
-        normalise(2, held[2])
-        normalise(3, held[3])
-        t2 = transposes(2)
-        z0 = recompute(0)
-        finish(2, t2)
+        normalise_saved(2)
         normalise(0, z0)
-        t3 = transposes(3)
-        z1 = recompute(1)
-        finish(3, t3)
+        t2 = transposes(2, 0)
+        normalise_saved(3)
         normalise(1, z1)
-        t0 = transposes(0)
+        t3 = transposes(3, 4)
+        finish(2, t2)
+        finish(3, t3)
+        t0 = transposes(0, 0)
         finish(0, t0)
-        t1 = transposes(1, last=True)
+        t1 = transposes(1, 4)
         finish(1, t1)

@@ -20,10 +20,11 @@ EPS_BN = 1e-5
 NEG_SLOPE = 0.01
 FLOPS = 2 * B * D * N * C
 
-VCOLS = [512, 512, 384, 256, 0, 0, 0, 0]
+VCOLS = [512, 512, 384, 256, 128, 0, 0, 0]
 STATS_LAG = 1
 STATS_PER_STEP = 2
 SAVED = [2, 3]
+ON_SCALAR = {0: 2, 1: 3}
 PIN = True
 
 
@@ -192,10 +193,10 @@ def tile_yuyipointupdate_pb_kernel(tc, h1, W2, g2, b2, out):
 
         ys = {}
 
-        def normalise(b, zs):
-            for ot in range(OT):
+        def normalise(b, zs, tiles):
+            for ot in tiles:
                 y = keep.tile([P, N], F32, name="y%d_%d" % (b, ot))
-                if ot < OT - 1:
+                if ot < ON_SCALAR[b]:
                     nc.scalar.activation(
                         out=y[:], in_=zs[ot][:], func=ACT.Identity,
                         bias=sh[:, ot : ot + 1], scale=sc[:, ot : ot + 1],
@@ -207,8 +208,8 @@ def tile_yuyipointupdate_pb_kernel(tc, h1, W2, g2, b2, out):
                     )
                 ys[(b, ot)] = y
 
-        def normalise_saved(b):
-            for ot in range(OT):
+        def normalise_saved(b, tiles):
+            for ot in tiles:
                 y = keep.tile([P, N], F32, name="y%d_%d" % (b, ot))
                 nc.vector.tensor_scalar(
                     out=y[:], in0=saved[(b, ot)][:], scalar1=sc[:, ot : ot + 1],
@@ -229,8 +230,8 @@ def tile_yuyipointupdate_pb_kernel(tc, h1, W2, g2, b2, out):
 
         outview = out.rearrange("b (j p) o -> b j p o", p=P)
 
-        def finish(b, ts):
-            for j in range(NJ):
+        def finish(b, ts, chunks):
+            for j in chunks:
                 a = apool.tile([P, D], F32, name="a")
                 nc.scalar.copy(out=a[:], in_=ts[j][:])
                 r = keep.tile([P, D], F32, name="r%d_%d" % (b, j))
@@ -239,15 +240,19 @@ def tile_yuyipointupdate_pb_kernel(tc, h1, W2, g2, b2, out):
                 )
                 nc.sync.dma_start(out=outview[b, j], in_=r[:])
 
-        normalise_saved(2)
-        normalise(0, z0)
+        every = [0, 1, 2, 3]
+        normalise_saved(2, every)
+        normalise(0, z0, every)
         t2 = transposes(2, 0)
-        normalise_saved(3)
-        normalise(1, z1)
+        finish(2, t2, [0, 1])
+        normalise_saved(3, [0, 1])
+        normalise(1, z1, [0])
+        finish(2, t2, [2, 3])
+        normalise_saved(3, [2, 3])
+        normalise(1, z1, [1, 2, 3])
         t3 = transposes(3, 4)
-        finish(2, t2)
-        finish(3, t3)
+        finish(3, t3, every)
         t0 = transposes(0, 0)
-        finish(0, t0)
+        finish(0, t0, every)
         t1 = transposes(1, 4)
-        finish(1, t1)
+        finish(1, t1, every)

@@ -193,8 +193,8 @@ def tile_yuyipointupdate_pb_kernel(tc, h1, W2, g2, b2, out):
 
         ys = {}
 
-        def normalise(b, zs, tiles):
-            for ot in tiles:
+        def normalise(b, zs):
+            for ot in range(OT):
                 y = keep.tile([P, N], F32, name="y%d_%d" % (b, ot))
                 if ot < ON_SCALAR[b]:
                     nc.scalar.activation(
@@ -208,8 +208,8 @@ def tile_yuyipointupdate_pb_kernel(tc, h1, W2, g2, b2, out):
                     )
                 ys[(b, ot)] = y
 
-        def normalise_saved(b, tiles):
-            for ot in tiles:
+        def normalise_saved(b):
+            for ot in range(OT):
                 y = keep.tile([P, N], F32, name="y%d_%d" % (b, ot))
                 nc.vector.tensor_scalar(
                     out=y[:], in0=saved[(b, ot)][:], scalar1=sc[:, ot : ot + 1],
@@ -230,8 +230,8 @@ def tile_yuyipointupdate_pb_kernel(tc, h1, W2, g2, b2, out):
 
         outview = out.rearrange("b (j p) o -> b j p o", p=P)
 
-        def finish(b, ts, chunks):
-            for j in chunks:
+        def finish(b, ts):
+            for j in range(NJ):
                 a = apool.tile([P, D], F32, name="a")
                 nc.scalar.copy(out=a[:], in_=ts[j][:])
                 r = keep.tile([P, D], F32, name="r%d_%d" % (b, j))
@@ -240,19 +240,15 @@ def tile_yuyipointupdate_pb_kernel(tc, h1, W2, g2, b2, out):
                 )
                 nc.sync.dma_start(out=outview[b, j], in_=r[:])
 
-        every = [0, 1, 2, 3]
-        normalise_saved(2, every)
-        normalise(0, z0, every)
+        normalise_saved(2)
+        normalise(0, z0)
         t2 = transposes(2, 0)
-        finish(2, t2, [0, 1])
-        normalise_saved(3, [0, 1])
-        normalise(1, z1, [0])
-        finish(2, t2, [2, 3])
-        normalise_saved(3, [2, 3])
-        normalise(1, z1, [1, 2, 3])
+        normalise_saved(3)
+        normalise(1, z1)
         t3 = transposes(3, 4)
-        finish(3, t3, every)
+        finish(2, t2)
+        finish(3, t3)
         t0 = transposes(0, 0)
-        finish(0, t0, every)
+        finish(0, t0)
         t1 = transposes(1, 4)
-        finish(1, t1, every)
+        finish(1, t1)

@@ -24,7 +24,7 @@ VCOLS = [512, 512, 384, 256, 128, 0, 0, 0]
 STATS_LAG = 1
 STATS_PER_STEP = 2
 SAVED = [2, 3]
-ON_SCALAR = {0: 2, 1: 3}
+ON_SCALAR = {0: 2, 1: 1}
 PIN = True
 
 
@@ -208,15 +208,6 @@ def tile_yuyipointupdate_pb_kernel(tc, h1, W2, g2, b2, out):
                     )
                 ys[(b, ot)] = y
 
-        def normalise_saved(b):
-            for ot in range(OT):
-                y = keep.tile([P, N], F32, name="y%d_%d" % (b, ot))
-                nc.vector.tensor_scalar(
-                    out=y[:], in0=saved[(b, ot)][:], scalar1=sc[:, ot : ot + 1],
-                    scalar2=sh[:, ot : ot + 1], op0=ALU.mult, op1=ALU.add,
-                )
-                ys[(b, ot)] = y
-
         def transposes(b, base):
             ts = []
             for j in range(NJ):
@@ -240,15 +231,59 @@ def tile_yuyipointupdate_pb_kernel(tc, h1, W2, g2, b2, out):
                 )
                 nc.sync.dma_start(out=outview[b, j], in_=r[:])
 
-        normalise_saved(2)
+        ms_ = {}
+
+        def normalise_gpsimd(b, ot):
+            y = keep.tile([P, N], F32, name="y%d_%d" % (b, ot))
+            nc.gpsimd.tensor_scalar(
+                out=y[:], in0=saved[(b, ot)][:], scalar1=sc[:, ot : ot + 1],
+                scalar2=sh[:, ot : ot + 1], op0=ALU.mult, op1=ALU.add,
+            )
+            ys[(b, ot)] = y
+
+        def negative_part(b, ot):
+            m = keep.tile([P, N], F32, name="m%d_%d" % (b, ot))
+            nc.gpsimd.tensor_scalar(
+                out=m[:], in0=ys[(b, ot)][:], scalar1=0.0, scalar2=NEG_SLOPE - 1.0, op0=ALU.min, op1=ALU.mult,
+            )
+            ms_[(b, ot)] = m
+
+        def transposes_sum(b, base):
+            ts = [bank(base + j, [P, D], "t%d_%d" % (b, j)) for j in range(NJ)]
+            for ot in range(OT):
+                for j in range(NJ):
+                    nc.tensor.matmul(
+                        ts[j][:, ot * P : (ot + 1) * P], lhsT=ys[(b, ot)][:, j * P : (j + 1) * P], rhs=ident[:],
+                        is_transpose=True, start=True, stop=False,
+                    )
+                for j in range(NJ):
+                    nc.tensor.matmul(
+                        ts[j][:, ot * P : (ot + 1) * P], lhsT=ms_[(b, ot)][:, j * P : (j + 1) * P], rhs=ident[:],
+                        is_transpose=True, start=False, stop=True,
+                    )
+            return ts
+
+        def finish_copy(b, ts):
+            for j in range(NJ):
+                r = keep.tile([P, D], F32, name="r%d_%d" % (b, j))
+                if j < NJ - 1:
+                    nc.scalar.copy(out=r[:], in_=ts[j][:])
+                else:
+                    nc.vector.tensor_copy(out=r[:], in_=ts[j][:])
+                nc.sync.dma_start(out=outview[b, j], in_=r[:])
+
+        for ot in range(OT):
+            normalise_gpsimd(3, ot)
         normalise(0, z0)
-        t2 = transposes(2, 0)
-        normalise_saved(3)
-        normalise(1, z1)
-        t3 = transposes(3, 4)
-        finish(2, t2)
-        finish(3, t3)
         t0 = transposes(0, 0)
-        finish(0, t0)
+        normalise(1, z1)
         t1 = transposes(1, 4)
+        for ot in range(OT):
+            normalise_gpsimd(2, ot)
+            negative_part(2, ot)
+        finish(0, t0)
+        t3 = transposes(3, 0)
         finish(1, t1)
+        t2 = transposes_sum(2, 4)
+        finish(3, t3)
+        finish_copy(2, t2)

@@ -24,7 +24,6 @@ VCOLS = [512, 512, 384, 256, 128, 0, 0, 0]
 STATS_LAG = 1
 STATS_PER_STEP = 2
 SAVED = [2, 3]
-ON_SCALAR = {0: 2, 1: 1}
 PIN = True
 
 
@@ -193,20 +192,19 @@ def tile_yuyipointupdate_pb_kernel(tc, h1, W2, g2, b2, out):
 
         ys = {}
 
-        def normalise(b, zs):
-            for ot in range(OT):
-                y = keep.tile([P, N], F32, name="y%d_%d" % (b, ot))
-                if ot < ON_SCALAR[b]:
-                    nc.scalar.activation(
-                        out=y[:], in_=zs[ot][:], func=ACT.Identity,
-                        bias=sh[:, ot : ot + 1], scale=sc[:, ot : ot + 1],
-                    )
-                else:
-                    nc.vector.tensor_scalar(
-                        out=y[:], in0=zs[ot][:], scalar1=sc[:, ot : ot + 1],
-                        scalar2=sh[:, ot : ot + 1], op0=ALU.mult, op1=ALU.add,
-                    )
-                ys[(b, ot)] = y
+        def normalise(b, zs, ot, on_scalar):
+            y = keep.tile([P, N], F32, name="y%d_%d" % (b, ot))
+            if on_scalar:
+                nc.scalar.activation(
+                    out=y[:], in_=zs[ot][:], func=ACT.Identity,
+                    bias=sh[:, ot : ot + 1], scale=sc[:, ot : ot + 1],
+                )
+            else:
+                nc.vector.tensor_scalar(
+                    out=y[:], in0=zs[ot][:], scalar1=sc[:, ot : ot + 1],
+                    scalar2=sh[:, ot : ot + 1], op0=ALU.mult, op1=ALU.add,
+                )
+            ys[(b, ot)] = y
 
         def transposes(b, base):
             ts = []
@@ -221,17 +219,14 @@ def tile_yuyipointupdate_pb_kernel(tc, h1, W2, g2, b2, out):
 
         outview = out.rearrange("b (j p) o -> b j p o", p=P)
 
-        def finish(b, ts):
-            for j in range(NJ):
-                a = apool.tile([P, D], F32, name="a")
-                nc.scalar.copy(out=a[:], in_=ts[j][:])
-                r = keep.tile([P, D], F32, name="r%d_%d" % (b, j))
-                nc.vector.scalar_tensor_tensor(
-                    out=r[:], in0=ts[j][:], scalar=NEG_SLOPE, in1=a[:], op0=ALU.mult, op1=ALU.max
-                )
-                nc.sync.dma_start(out=outview[b, j], in_=r[:])
-
-        ms_ = {}
+        def finish(b, ts, j):
+            a = apool.tile([P, D], F32, name="a")
+            nc.scalar.copy(out=a[:], in_=ts[j][:])
+            r = keep.tile([P, D], F32, name="r%d_%d" % (b, j))
+            nc.vector.scalar_tensor_tensor(
+                out=r[:], in0=ts[j][:], scalar=NEG_SLOPE, in1=a[:], op0=ALU.mult, op1=ALU.max
+            )
+            nc.sync.dma_start(out=outview[b, j], in_=r[:])
 
         def normalise_gpsimd(b, ot):
             y = keep.tile([P, N], F32, name="y%d_%d" % (b, ot))
@@ -241,49 +236,25 @@ def tile_yuyipointupdate_pb_kernel(tc, h1, W2, g2, b2, out):
             )
             ys[(b, ot)] = y
 
-        def negative_part(b, ot):
-            m = keep.tile([P, N], F32, name="m%d_%d" % (b, ot))
-            nc.gpsimd.tensor_scalar(
-                out=m[:], in0=ys[(b, ot)][:], scalar1=0.0, scalar2=NEG_SLOPE - 1.0, op0=ALU.min, op1=ALU.mult,
-            )
-            ms_[(b, ot)] = m
-
-        def transposes_sum(b, base):
-            ts = [bank(base + j, [P, D], "t%d_%d" % (b, j)) for j in range(NJ)]
+        for b in (2, 3):
             for ot in range(OT):
-                for j in range(NJ):
-                    nc.tensor.matmul(
-                        ts[j][:, ot * P : (ot + 1) * P], lhsT=ys[(b, ot)][:, j * P : (j + 1) * P], rhs=ident[:],
-                        is_transpose=True, start=True, stop=False,
-                    )
-                for j in range(NJ):
-                    nc.tensor.matmul(
-                        ts[j][:, ot * P : (ot + 1) * P], lhsT=ms_[(b, ot)][:, j * P : (j + 1) * P], rhs=ident[:],
-                        is_transpose=True, start=False, stop=True,
-                    )
-            return ts
-
-        def finish_copy(b, ts):
-            for j in range(NJ):
-                r = keep.tile([P, D], F32, name="r%d_%d" % (b, j))
-                if j < NJ - 1:
-                    nc.scalar.copy(out=r[:], in_=ts[j][:])
-                else:
-                    nc.vector.tensor_copy(out=r[:], in_=ts[j][:])
-                nc.sync.dma_start(out=outview[b, j], in_=r[:])
-
+                normalise_gpsimd(b, ot)
         for ot in range(OT):
-            normalise_gpsimd(3, ot)
-        normalise(0, z0)
+            normalise(0, z0, ot, ot < 2)
         t0 = transposes(0, 0)
-        normalise(1, z1)
+        normalise(1, z1, 0, True)
+        normalise(1, z1, 2, False)
+        normalise(1, z1, 3, False)
+        finish(0, t0, 0)
+        normalise(1, z1, 1, True)
         t1 = transposes(1, 4)
-        for ot in range(OT):
-            normalise_gpsimd(2, ot)
-            negative_part(2, ot)
-        finish(0, t0)
-        t3 = transposes(3, 0)
-        finish(1, t1)
-        t2 = transposes_sum(2, 4)
-        finish(3, t3)
-        finish_copy(2, t2)
+        for j in range(1, NJ):
+            finish(0, t0, j)
+        t2 = transposes(2, 0)
+        for j in range(NJ):
+            finish(1, t1, j)
+        t3 = transposes(3, 4)
+        for j in range(NJ):
+            finish(2, t2, j)
+        for j in range(NJ):
+            finish(3, t3, j)

@@ -20,7 +20,7 @@ EPS_BN = 1e-5
 NEG_SLOPE = 0.01
 FLOPS = 2 * B * D * N * C
 
-VCOLS = [512, 512, 384, 256, 128, 0, 0, 0]
+VCOLS = [160, 512, 256, 128, 128, 0, 0, 0]
 STATS_LAG = 1
 STATS_PER_STEP = 2
 SAVED = [2, 3]
@@ -46,7 +46,7 @@ def tile_yuyipointupdate_pb_kernel(tc, h1, W2, g2, b2, out):
         one = keep.tile([P, 1], F32, name="one")
         nc.vector.memset(one[:], 1.0)
         warm = keep.tile([P, 1], F32, name="warm")
-        nc.scalar.activation(out=warm[:], in_=one[:], func=ACT.Sqrt)
+        nc.scalar.activation(out=warm[:], in_=one[:], func=ACT.Abs_reciprocal_sqrt)
         ident = keep.tile([P, P], F32, name="ident")
         masks.make_identity(nc, ident[:])
 
@@ -69,8 +69,8 @@ def tile_yuyipointupdate_pb_kernel(tc, h1, W2, g2, b2, out):
         w2words = w2raw[:].bitcast(F32).rearrange("p t (g q u) -> p t g u q", g=G, u=2)
         w2grpw = w2grp[:].bitcast(F32)
 
-        def w2_stage():
-            nc.vector.tensor_copy(out=gbf[:], in_=gbraw[:])
+        def w2_turn():
+            nc.gpsimd.tensor_copy(out=gbf[:], in_=gbraw[:])
             for ot in range(OT):
                 wt = bank(ot, [P, G, 2, P], "wt%d" % ot)
                 for g in range(G):
@@ -79,13 +79,14 @@ def tile_yuyipointupdate_pb_kernel(tc, h1, W2, g2, b2, out):
                 nc.scalar.copy(out=w2grpw[:, ot], in_=wt[:].rearrange("p g u o -> p g o u"))
             gbps = bank(4, [P, P], "gbps")
             nc.tensor.transpose(gbps[:], gbf[:], ident[:])
-            for ot in range(OT):
-                nc.vector.quantize_mx(
-                    out=w2codes[:, ot].rearrange("p g o -> p (g o)").bitcast(FP8X4),
-                    scales=w2scales[:, ot].rearrange("p g o -> p (g o)"),
-                    in_=w2grp[:, ot].rearrange("p g o t -> p (g o t)"),
-                )
-            nc.vector.tensor_copy(out=gb[:], in_=gbps[:, 0 : 2 * OT])
+            nc.scalar.copy(out=gb[:], in_=gbps[:, 0 : 2 * OT])
+
+        def w2_quantise(ot):
+            nc.vector.quantize_mx(
+                out=w2codes[:, ot].rearrange("p g o -> p (g o)").bitcast(FP8X4),
+                scales=w2scales[:, ot].rearrange("p g o -> p (g o)"),
+                in_=w2grp[:, ot].rearrange("p g o t -> p (g o t)"),
+            )
 
         h1codes = keep.tile([P, B * G, N], U32, name="h1codes", align_bytes=64)
         h1scales = keep.tile([P, B * G, N], U8, name="h1scales", align_bytes=64)
@@ -127,23 +128,29 @@ def tile_yuyipointupdate_pb_kernel(tc, h1, W2, g2, b2, out):
         held = {}
         saved = {}
 
-        def save(b):
-            for ot in range(OT):
-                zs = keep.tile([P, N], F32, name="zs%d_%d" % (b, ot))
-                nc.scalar.copy(out=zs[:], in_=held[b][ot][:])
-                saved[(b, ot)] = zs
+        def save(b, ot):
+            zs = keep.tile([P, N], F32, name="zs%d_%d" % (b, ot))
+            nc.scalar.copy(out=zs[:], in_=held[b][ot][:])
+            saved[(b, ot)] = zs
 
         units = []
         taken = 0
-        for k in range(B * G + 1):
-            if k < B * G:
+        regroup(0)
+        w2_turn()
+        quantise(0)
+        w2_quantise(0)
+        w2_quantise(1)
+        regroup(1)
+        w2_quantise(2)
+        w2_quantise(3)
+        for k in range(1, B * G + 1):
+            if 2 <= k < B * G:
                 regroup(k)
-            if k == 1:
-                w2_stage()
             if k >= 1:
                 c = k - 1
                 b, g = c // G, c % G
-                quantise(c)
+                if c >= 1:
+                    quantise(c)
                 if g == 0:
                     base = 4 if b % 2 == 0 else 0
                     held[b] = [bank(base + ot, [P, N], "z%d_%d" % (b, ot)) for ot in range(OT)]
@@ -152,18 +159,18 @@ def tile_yuyipointupdate_pb_kernel(tc, h1, W2, g2, b2, out):
                 if g == G - 1:
                     units.extend([(c, b, ot) for ot in range(OT)])
             last = k == B * G
-            if k == B * G - 1:
-                save(2)
-            if last:
-                save(3)
             for w in units[taken : (len(units) if last else taken + STATS_PER_STEP)]:
                 if last or w[0] <= k - 1 - STATS_LAG:
-                    src = saved[(w[1], w[2])] if w[1] in SAVED else held[w[1]][w[2]]
-                    nc.vector.bn_stats(out=stats[:, w[2], w[1], :], in_=src[:])
+                    nc.vector.bn_stats(out=stats[:, w[2], w[1], :], in_=held[w[1]][w[2]][:])
                     taken += 1
                     if w[1] == B - 1 and w[2] > 0:
                         aggregate(w[2] - 1)
+                    if w[1] in SAVED and w != units[-1]:
+                        save(w[1], w[2])
         aggregate(OT - 1)
+        rstd = keep.tile([P, OT], F32, name="rstd")
+        nc.scalar.activation(out=rstd[:], in_=mv[:, :, 1], func=ACT.Abs_reciprocal_sqrt, bias=EPS_BN, scale=1.0)
+        save(B - 1, OT - 1)
 
         def recompute(b, base):
             zs = [bank(base + ot, [P, N], "zr%d_%d" % (b, ot)) for ot in range(OT)]
@@ -175,14 +182,10 @@ def tile_yuyipointupdate_pb_kernel(tc, h1, W2, g2, b2, out):
         z1 = recompute(1, 4)
         z0 = recompute(0, 0)
 
-        sd = keep.tile([P, OT], F32, name="sd")
-        nc.scalar.activation(out=sd[:], in_=mv[:, :, 1], func=ACT.Sqrt, bias=EPS_BN, scale=1.0)
         mg = keep.tile([P, OT], F32, name="mg")
         nc.vector.scalar_tensor_tensor(
             out=mg[:], in0=mv[:, :, 0], scalar=-1.0, in1=gb[:, 0:OT], op0=ALU.mult, op1=ALU.mult
         )
-        rstd = keep.tile([P, OT], F32, name="rstd")
-        nc.vector.reciprocal(out=rstd[:], in_=sd[:])
         ms = keep.tile([P, OT], F32, name="ms")
         nc.vector.tensor_tensor(out=ms[:], in0=mg[:], in1=rstd[:], op=ALU.mult)
         sc = keep.tile([P, OT], F32, name="sc")
@@ -240,20 +243,20 @@ def tile_yuyipointupdate_pb_kernel(tc, h1, W2, g2, b2, out):
             for ot in range(OT):
                 normalise_gpsimd(b, ot)
         for ot in range(OT):
-            normalise(0, z0, ot, ot < 2)
-        t0 = transposes(0, 0)
-        normalise(1, z1, 0, True)
-        normalise(1, z1, 2, False)
-        normalise(1, z1, 3, False)
-        finish(0, t0, 0)
-        normalise(1, z1, 1, True)
+            normalise(1, z1, ot, ot < 2)
         t1 = transposes(1, 4)
+        normalise(0, z0, 0, True)
+        normalise(0, z0, 2, False)
+        normalise(0, z0, 3, False)
+        finish(1, t1, 0)
+        normalise(0, z0, 1, True)
+        t0 = transposes(0, 0)
         for j in range(1, NJ):
-            finish(0, t0, j)
-        t2 = transposes(2, 0)
-        for j in range(NJ):
             finish(1, t1, j)
-        t3 = transposes(3, 4)
+        t2 = transposes(2, 4)
+        for j in range(NJ):
+            finish(0, t0, j)
+        t3 = transposes(3, 0)
         for j in range(NJ):
             finish(2, t2, j)
         for j in range(NJ):

@@ -93,12 +93,12 @@ def tile_yuyipointupdate_pb_kernel(tc, h1, W2, g2, b2, out):
         grps = [keep.tile([P, N, 4], BF16, name="h1grp%d" % k, align_bytes=64) for k in range(B * G)]
 
         def regroup(k):
-            dst = grps[k][:].rearrange("p (c i) t -> p c t i", i=4)
-            src = h1raw[k][:].rearrange("p t (c i) -> p c t i", i=4)
-            cv = VCOLS[k] // 4
+            dst = grps[k][:].rearrange("p (c i) t -> p c t i", i=8)
+            src = h1raw[k][:].rearrange("p t (c i) -> p c t i", i=8)
+            cv = VCOLS[k] // 8
             if cv > 0:
                 nc.vector.tensor_copy(out=dst[:, 0:cv], in_=src[:, 0:cv])
-            if cv < N // 4:
+            if cv < N // 8:
                 nc.scalar.copy(out=dst[:, cv:], in_=src[:, cv:])
 
         def quantise(k):

@@ -25,6 +25,7 @@ STATS_LAG = 1
 STATS_PER_STEP = 2
 SAVED = [2, 3]
 PIN = True
+SINGLES = [(3, 1)]
 
 
 def tile_yuyipointupdate_pb_kernel(tc, h1, W2, g2, b2, out):
@@ -93,8 +94,8 @@ def tile_yuyipointupdate_pb_kernel(tc, h1, W2, g2, b2, out):
         grps = [keep.tile([P, N, 4], BF16, name="h1grp%d" % k, align_bytes=64) for k in range(B * G)]
 
         def regroup(k):
-            dst = grps[k][:].rearrange("p (c i) t -> p c t i", i=8)
-            src = h1raw[k][:].rearrange("p t (c i) -> p c t i", i=8)
+            dst = grps[k][:].rearrange("p (j c i) t -> p c t i j", j=2, i=4)
+            src = h1raw[k][:].rearrange("p t (c i j) -> p c t i j", i=4, j=2)
             cv = VCOLS[k] // 8
             if cv > 0:
                 nc.vector.tensor_copy(out=dst[:, 0:cv], in_=src[:, 0:cv])
@@ -210,26 +211,33 @@ def tile_yuyipointupdate_pb_kernel(tc, h1, W2, g2, b2, out):
             ys[(b, ot)] = y
 
         def transposes(b, base):
-            ts = []
-            for j in range(NJ):
+            ts = {}
+            for j in (0, 2, 1, 3):
                 t = bank(base + j, [P, D], "t%d_%d" % (b, j))
                 for ot in range(OT):
                     nc.tensor.transpose(
                         t[:, ot * P : (ot + 1) * P], ys[(b, ot)][:, j * P : (j + 1) * P], ident[:]
                     )
-                ts.append(t)
+                ts[j] = t
             return ts
 
-        outview = out.rearrange("b (j p) o -> b j p o", p=P)
+        outview = out.rearrange("b (h p e) o -> b h p e o", h=2, e=2)
+        pairs = {}
 
         def finish(b, ts, j):
+            h, e = j // 2, j % 2
             a = apool.tile([P, D], F32, name="a")
-            nc.scalar.copy(out=a[:], in_=ts[j][:])
-            r = keep.tile([P, D], F32, name="r%d_%d" % (b, j))
+            nc.scalar.copy(out=a[:], in_=ts[2 * e + h][:])
+            if e == 0:
+                pairs[(b, h)] = keep.tile([P, 2, D], F32, name="r%d_%d" % (b, h))
+            r = pairs[(b, h)]
             nc.vector.scalar_tensor_tensor(
-                out=r[:], in0=ts[j][:], scalar=NEG_SLOPE, in1=a[:], op0=ALU.mult, op1=ALU.max
+                out=r[:, e, :], in0=ts[2 * e + h][:], scalar=NEG_SLOPE, in1=a[:], op0=ALU.mult, op1=ALU.max
             )
-            nc.sync.dma_start(out=outview[b, j], in_=r[:])
+            if (b, h) in SINGLES:
+                nc.sync.dma_start(out=outview[b, h, :, e], in_=r[:, e, :])
+            elif e == 1:
+                nc.sync.dma_start(out=outview[b, h], in_=r[:])
 
         def normalise_gpsimd(b, ot):
             y = keep.tile([P, N], F32, name="y%d_%d" % (b, ot))

@@ -25,7 +25,7 @@ STATS_LAG = 1
 STATS_PER_STEP = 2
 SAVED = [2, 3]
 PIN = True
-SINGLES = [(3, 1)]
+SINGLES = [(1, 0), (3, 1)]
 
 
 def tile_yuyipointupdate_pb_kernel(tc, h1, W2, g2, b2, out):
@@ -256,8 +256,8 @@ def tile_yuyipointupdate_pb_kernel(tc, h1, W2, g2, b2, out):
         normalise(0, z0, 0, True)
         normalise(0, z0, 2, False)
         normalise(0, z0, 3, False)
+        normalise(0, z0, 1, False)
         finish(1, t1, 0)
-        normalise(0, z0, 1, True)
         t0 = transposes(0, 0)
         for j in range(1, NJ):
             finish(1, t1, j)

from contextlib import ExitStack

import concourse.masks as masks
import concourse.mybir as mybir

F32 = mybir.dt.float32
BF16 = mybir.dt.bfloat16
U32 = mybir.dt.uint32
U8 = mybir.dt.uint8
FP8X4 = mybir.dt.float8_e4m3fn_x4
ACT = mybir.ActivationFunctionType
ALU = mybir.AluOpType

P = 128
B, C, N, D = 4, 1024, 512, 512
G = C // 512
OT = D // P
NJ = N // P
EPS_BN = 1e-5
NEG_SLOPE = 0.01
FLOPS = 2 * B * D * N * C

VCOLS = [160, 512, 256, 128, 128, 0, 0, 0]
STATS_LAG = 1
STATS_PER_STEP = 2
SAVED = [2, 3]
PIN = True
SINGLES = [(1, 0), (3, 1)]


def tile_yuyipointupdate_pb_kernel(tc, h1, W2, g2, b2, out):
    nc = tc.nc
    with ExitStack() as ctx:
        keep = ctx.enter_context(tc.tile_pool(name="keep", bufs=1))
        apool = ctx.enter_context(tc.tile_pool(name="apool", bufs=4))
        psum = ctx.enter_context(tc.psum_pool(name="psum", bufs=1))
        if PIN:
            ctx.enter_context(tc.manual_schedule())

        def bank(i, shape, name):
            return psum.tile(shape, F32, tag="bank%d" % i, name=name)

        gbraw = keep.tile([P, P], BF16, name="gbraw")
        nc.vector.memset(gbraw[:], 0.0)
        nc.scalar.dma_start(out=gbraw[0:OT, :], in_=g2.rearrange("(t p) -> t p", p=P))
        nc.scalar.dma_start(out=gbraw[OT : 2 * OT, :], in_=b2.rearrange("(t p) -> t p", p=P))
        one = keep.tile([P, 1], F32, name="one")
        nc.vector.memset(one[:], 1.0)
        warm = keep.tile([P, 1], F32, name="warm")
        nc.scalar.activation(out=warm[:], in_=one[:], func=ACT.Abs_reciprocal_sqrt)
        ident = keep.tile([P, P], F32, name="ident")
        masks.make_identity(nc, ident[:])

        w2raw = keep.tile([P, OT, C], BF16, name="w2raw")
        w2view = W2.rearrange("(t p) c -> p t c", p=P)
        h1view = h1.rearrange("b (g p j) n -> b g p j n", g=G, p=P, j=4)
        h1raw = [keep.tile([P, 4, N], BF16, name="h1raw%d" % k) for k in range(B * G)]
        nc.sync.dma_start(out=h1raw[0][:], in_=h1view[0, 0])
        nc.sync.dma_start(out=w2raw[:, 0:2, :], in_=w2view[:, 0:2, :])
        nc.sync.dma_start(out=w2raw[:, 2:4, :], in_=w2view[:, 2:4, :])
        for k in range(1, B * G):
            nc.sync.dma_start(out=h1raw[k][:], in_=h1view[k // G, k % G])

        gbf = keep.tile([P, P], F32, name="gbf")
        gb = keep.tile([P, 2 * OT], F32, name="gb")

        w2grp = keep.tile([P, OT, G, P, 4], BF16, name="w2grp", align_bytes=64)
        w2codes = keep.tile([P, OT, G, P], U32, name="w2codes", align_bytes=64)
        w2scales = keep.tile([P, OT, G, P], U8, name="w2scales", align_bytes=64)
        w2words = w2raw[:].bitcast(F32).rearrange("p t (g q u) -> p t g u q", g=G, u=2)
        w2grpw = w2grp[:].bitcast(F32)

        def w2_turn():
            nc.gpsimd.tensor_copy(out=gbf[:], in_=gbraw[:])
            for ot in range(OT):
                wt = bank(ot, [P, G, 2, P], "wt%d" % ot)
                for g in range(G):
                    for u in range(2):
                        nc.tensor.transpose(wt[:, g, u, :], w2words[:, ot, g, u, :], ident[:])
                nc.scalar.copy(out=w2grpw[:, ot], in_=wt[:].rearrange("p g u o -> p g o u"))
            gbps = bank(4, [P, P], "gbps")
            nc.tensor.transpose(gbps[:], gbf[:], ident[:])
            nc.scalar.copy(out=gb[:], in_=gbps[:, 0 : 2 * OT])

        def w2_quantise(ot):
            nc.vector.quantize_mx(
                out=w2codes[:, ot].rearrange("p g o -> p (g o)").bitcast(FP8X4),
                scales=w2scales[:, ot].rearrange("p g o -> p (g o)"),
                in_=w2grp[:, ot].rearrange("p g o t -> p (g o t)"),
            )

        h1codes = keep.tile([P, B * G, N], U32, name="h1codes", align_bytes=64)
        h1scales = keep.tile([P, B * G, N], U8, name="h1scales", align_bytes=64)
        grps = [keep.tile([P, N, 4], BF16, name="h1grp%d" % k, align_bytes=64) for k in range(B * G)]

        def regroup(k):
            dst = grps[k][:].rearrange("p (j c i) t -> p c t i j", j=2, i=4)
            src = h1raw[k][:].rearrange("p t (c i j) -> p c t i j", i=4, j=2)
            cv = VCOLS[k] // 8
            if cv > 0:
                nc.vector.tensor_copy(out=dst[:, 0:cv], in_=src[:, 0:cv])
            if cv < N // 8:
                nc.scalar.copy(out=dst[:, cv:], in_=src[:, cv:])

        def quantise(k):
            nc.vector.quantize_mx(
                out=h1codes[:, k, :].bitcast(FP8X4),
                scales=h1scales[:, k, :],
                in_=grps[k][:].rearrange("p n t -> p (n t)"),
            )

        def mx_pass(z, b, ot, g):
            nc.tensor.matmul_mx(
                out=z[:],
                lhsT=w2codes[:, ot, g, :].bitcast(FP8X4),
                lhsT_scale=w2scales[:, ot, g, :],
                rhs=h1codes[:, b * G + g, :].bitcast(FP8X4),
                rhs_scale=h1scales[:, b * G + g, :],
                start=(g == 0),
                stop=(g == G - 1),
            )

        stats = keep.tile([P, OT, B, 6], F32, name="stats")
        mv = keep.tile([P, OT, 2], F32, name="mv")

        def aggregate(ot):
            nc.vector.bn_aggr(out=mv[:, ot, :], in_=stats[:, ot].rearrange("p b s -> p (b s)"))

        held = {}
        saved = {}

        def save(b, ot):
            zs = keep.tile([P, N], F32, name="zs%d_%d" % (b, ot))
            nc.scalar.copy(out=zs[:], in_=held[b][ot][:])
            saved[(b, ot)] = zs

        units = []
        taken = 0
        regroup(0)
        w2_turn()
        quantise(0)
        w2_quantise(0)
        w2_quantise(1)
        regroup(1)
        w2_quantise(2)
        w2_quantise(3)
        for k in range(1, B * G + 1):
            if 2 <= k < B * G:
                regroup(k)
            if k >= 1:
                c = k - 1
                b, g = c // G, c % G
                if c >= 1:
                    quantise(c)
                if g == 0:
                    base = 4 if b % 2 == 0 else 0
                    held[b] = [bank(base + ot, [P, N], "z%d_%d" % (b, ot)) for ot in range(OT)]
                for ot in range(OT):
                    mx_pass(held[b][ot], b, ot, g)
                if g == G - 1:
                    units.extend([(c, b, ot) for ot in range(OT)])
            last = k == B * G
            for w in units[taken : (len(units) if last else taken + STATS_PER_STEP)]:
                if last or w[0] <= k - 1 - STATS_LAG:
                    nc.vector.bn_stats(out=stats[:, w[2], w[1], :], in_=held[w[1]][w[2]][:])
                    taken += 1
                    if w[1] == B - 1 and w[2] > 0:
                        aggregate(w[2] - 1)
                    if w[1] in SAVED and w != units[-1]:
                        save(w[1], w[2])
        aggregate(OT - 1)
        rstd = keep.tile([P, OT], F32, name="rstd")
        nc.scalar.activation(out=rstd[:], in_=mv[:, :, 1], func=ACT.Abs_reciprocal_sqrt, bias=EPS_BN, scale=1.0)
        save(B - 1, OT - 1)

        def recompute(b, base):
            zs = [bank(base + ot, [P, N], "zr%d_%d" % (b, ot)) for ot in range(OT)]
            for ot in range(OT):
                for g in range(G):
                    mx_pass(zs[ot], b, ot, g)
            return zs

        z1 = recompute(1, 4)
        z0 = recompute(0, 0)

        mg = keep.tile([P, OT], F32, name="mg")
        nc.vector.scalar_tensor_tensor(
            out=mg[:], in0=mv[:, :, 0], scalar=-1.0, in1=gb[:, 0:OT], op0=ALU.mult, op1=ALU.mult
        )
        ms = keep.tile([P, OT], F32, name="ms")
        nc.vector.tensor_tensor(out=ms[:], in0=mg[:], in1=rstd[:], op=ALU.mult)
        sc = keep.tile([P, OT], F32, name="sc")
        nc.vector.tensor_tensor(out=sc[:], in0=gb[:, 0:OT], in1=rstd[:], op=ALU.mult)
        sh = keep.tile([P, OT], F32, name="sh")
        nc.vector.tensor_tensor(out=sh[:], in0=ms[:], in1=gb[:, OT : 2 * OT], op=ALU.add)

        ys = {}

        def normalise(b, zs, ot, on_scalar):
            y = keep.tile([P, N], F32, name="y%d_%d" % (b, ot))
            if on_scalar:
                nc.scalar.activation(
                    out=y[:], in_=zs[ot][:], func=ACT.Identity,
                    bias=sh[:, ot : ot + 1], scale=sc[:, ot : ot + 1],
                )
            else:
                nc.vector.tensor_scalar(
                    out=y[:], in0=zs[ot][:], scalar1=sc[:, ot : ot + 1],
                    scalar2=sh[:, ot : ot + 1], op0=ALU.mult, op1=ALU.add,
                )
            ys[(b, ot)] = y

        def transposes(b, base):
            ts = {}
            for j in (0, 2, 1, 3):
                t = bank(base + j, [P, D], "t%d_%d" % (b, j))
                for ot in range(OT):
                    nc.tensor.transpose(
                        t[:, ot * P : (ot + 1) * P], ys[(b, ot)][:, j * P : (j + 1) * P], ident[:]
                    )
                ts[j] = t
            return ts

        outview = out.rearrange("b (h p e) o -> b h p e o", h=2, e=2)
        pairs = {}

        def finish(b, ts, j):
            h, e = j // 2, j % 2
            a = apool.tile([P, D], F32, name="a")
            nc.scalar.copy(out=a[:], in_=ts[2 * e + h][:])
            if e == 0:
                pairs[(b, h)] = keep.tile([P, 2, D], F32, name="r%d_%d" % (b, h))
            r = pairs[(b, h)]
            nc.vector.scalar_tensor_tensor(
                out=r[:, e, :], in0=ts[2 * e + h][:], scalar=NEG_SLOPE, in1=a[:], op0=ALU.mult, op1=ALU.max
            )
            if (b, h) in SINGLES:
                nc.sync.dma_start(out=outview[b, h, :, e], in_=r[:, e, :])
            elif e == 1:
                nc.sync.dma_start(out=outview[b, h], in_=r[:])

        def normalise_gpsimd(b, ot):
            y = keep.tile([P, N], F32, name="y%d_%d" % (b, ot))
            nc.gpsimd.tensor_scalar(
                out=y[:], in0=saved[(b, ot)][:], scalar1=sc[:, ot : ot + 1],
                scalar2=sh[:, ot : ot + 1], op0=ALU.mult, op1=ALU.add,
            )
            ys[(b, ot)] = y

        for b in (2, 3):
            for ot in range(OT):
                normalise_gpsimd(b, ot)
        for ot in range(OT):
            normalise(1, z1, ot, ot < 2)
        t1 = transposes(1, 4)
        normalise(0, z0, 0, True)
        normalise(0, z0, 2, False)
        normalise(0, z0, 3, False)
        normalise(0, z0, 1, False)
        finish(1, t1, 0)
        t0 = transposes(0, 0)
        for j in range(1, NJ):
            finish(1, t1, j)
        t2 = transposes(2, 4)
        for j in range(NJ):
            finish(0, t0, j)
        t3 = transposes(3, 0)
        for j in range(NJ):
            finish(2, t2, j)
        for j in range(NJ):
            finish(3, t3, j)
